import numpy as np
import ml_dtypes

BF16 = ml_dtypes.bfloat16


def bf(x):
    return np.asarray(x, np.float32).astype(BF16)


def f32(x):
    return np.asarray(x, np.float32)


def f64(x):
    return np.asarray(x).astype(np.float64)


def striped(idx):
    return np.tile(idx.reshape(-1, 16).T, (8, 1))


E, C, S, N = 1024, 512, 512, 128
EPS = 1e-6


def setup_inputs():
    h = np.random.standard_normal((E, N)) * (0.5 + 1.5 * np.random.random((1, N)))
    return {"h": f32(h), "ln_w": f32(0.1 * np.random.standard_normal((E, 1))), "wv": bf(np.random.standard_normal((E, C)) / np.sqrt(E)), "base": f32(np.random.standard_normal((C, S))), "offs": striped(np.random.permutation(S)[:N])}


def reference(h, ln_w, wv, base, offs):
    idx = offs[:16].T.reshape(-1)
    hh = f64(h)
    r = 1.0 / np.sqrt(np.mean(hh * hh, axis=0, keepdims=True) + EPS)
    p = f64(wv).T @ (hh * (1.0 + f64(ln_w)))
    out = f64(base).copy()
    out[:, idx] = p * r
    return out

@@ -1,0 +1,73 @@
+import concourse.mybir as mybir
+
+F32 = mybir.dt.float32
+BF16 = mybir.dt.bfloat16
+U16 = mybir.dt.uint16
+MULT = mybir.AluOpType.mult
+SQUARE = mybir.ActivationFunctionType.Square
+SQRT = mybir.ActivationFunctionType.Sqrt
+
+P = 128
+E, C, S, N = 1024, 512, 512, 128
+KB = E // P
+CB = C // P
+EPS = 1e-6
+
+FLOPS = 2 * E * C * N + 2 * E * N
+
+
+def tile_gemmaforcausallm_kernel(tc, h, ln_w, wv, base, offs, out):
+    nc = tc.nc
+    with (
+        tc.tile_pool(name="held", bufs=1) as held,
+        tc.psum_pool(name="psum", bufs=1) as psum,
+    ):
+        offsets = held.tile([P, N // 16], U16, name="offsets")
+        nc.sync.dma_start(offsets[:], offs)
+        lnw_sb = held.tile([P, KB], F32, name="lnw_sb")
+        nc.sync.dma_start(lnw_sb[:], ln_w.rearrange("(p k) o -> p (k o)", k=KB))
+        h_sb = held.tile([P, KB, N], F32, name="h_sb")
+        nc.sync.dma_start(h_sb[:], h.rearrange("(p k) j -> p k j", k=KB))
+        wv_sb = held.tile([P, KB, C], BF16, name="wv_sb")
+        nc.sync.dma_start(wv_sb[:], wv.rearrange("(p k) c -> p k c", k=KB))
+        windows = []
+        for b in range(CB):
+            window = held.tile([P, S], F32, name=f"window{b}")
+            nc.sync.dma_start(window[:], base[b * P : (b + 1) * P, :])
+            windows.append(window)
+
+        ones = held.tile([P, P], BF16, name="ones")
+        nc.vector.memset(ones[:], 1.0)
+        eps = held.tile([P, 1], F32, name="eps")
+        nc.vector.memset(eps[:], EPS)
+
+        gain = held.tile([P, KB], F32, name="gain")
+        nc.vector.tensor_scalar_add(gain[:], lnw_sb[:], 1.0)
+        hs = held.tile([P, KB, N], BF16, name="hs")
+        for k in range(KB):
+            nc.vector.tensor_scalar_mul(hs[:, k, :], h_sb[:, k, :], gain[:, k : k + 1])
+
+        sq = held.tile([P, KB, N], BF16, name="sq")
+        nc.scalar.activation(sq[:], h_sb[:], SQUARE)
+        ssq = psum.tile([P, N], F32, name="ssq")
+        for k in range(KB):
+            nc.tensor.matmul(ssq[:], ones[:], sq[:, k, :], start=(k == 0), stop=(k == KB - 1))
+        rms = held.tile([P, N], F32, name="rms")
+        nc.scalar.activation(rms[:], ssq[:], SQRT, bias=eps[:], scale=1.0 / E)
+        r = held.tile([P, N], F32, name="r")
+        nc.vector.reciprocal(r[:], rms[:])
+
+        for b in range(CB):
+            proj = psum.tile([P, N], F32, name=f"proj{b}")
+            for k in range(KB):
+                nc.tensor.matmul(
+                    proj[:],
+                    wv_sb[:, k, b * P : (b + 1) * P],
+                    hs[:, k, :],
+                    start=(k == 0),
+                    stop=(k == KB - 1),
+                )
+            proj_sb = held.tile([P, N], F32, name=f"proj_sb{b}")
+            nc.scalar.copy(proj_sb[:], proj[:])
+            nc.vector.tensor_tensor(windows[b][:].indirect(offsets[:]), proj_sb[:], r[:], MULT)
+            nc.sync.dma_start(out[b * P : (b + 1) * P, :], windows[b][:])

@@ -11,6 +11,8 @@ P = 128
 E, C, S, N = 1024, 512, 512, 128
 KB = E // P
 CB = C // P
+HC = 4
+KC = KB // HC
 EPS = 1e-6
 
 FLOPS = 2 * E * C * N + 2 * E * N
@@ -18,40 +20,53 @@ FLOPS = 2 * E * C * N + 2 * E * N
 
 def tile_gemmaforcausallm_kernel(tc, h, ln_w, wv, base, offs, out):
     nc = tc.nc
+    h_view = h.rearrange("(p k) j -> p k j", k=KB)
+    wv_view = wv.rearrange("(p k) c -> p k c", k=KB)
     with (
         tc.tile_pool(name="held", bufs=1) as held,
         tc.psum_pool(name="psum", bufs=1) as psum,
     ):
+        lnw_sb = held.tile([P, KB], F32, name="lnw_sb")
+        nc.scalar.dma_start(lnw_sb[:], ln_w.rearrange("(p k) o -> p (k o)", k=KB))
+        h_chunks = []
+        for i in range(HC):
+            h_chunk = held.tile([P, KC, N], F32, name=f"h_chunk{i}")
+            nc.sync.dma_start(h_chunk[:], h_view[:, i * KC : (i + 1) * KC, :])
+            h_chunks.append(h_chunk)
         offsets = held.tile([P, N // 16], U16, name="offsets")
         nc.sync.dma_start(offsets[:], offs)
-        lnw_sb = held.tile([P, KB], F32, name="lnw_sb")
-        nc.sync.dma_start(lnw_sb[:], ln_w.rearrange("(p k) o -> p (k o)", k=KB))
-        h_sb = held.tile([P, KB, N], F32, name="h_sb")
-        nc.sync.dma_start(h_sb[:], h.rearrange("(p k) j -> p k j", k=KB))
-        wv_sb = held.tile([P, KB, C], BF16, name="wv_sb")
-        nc.sync.dma_start(wv_sb[:], wv.rearrange("(p k) c -> p k c", k=KB))
-        windows = []
-        for b in range(CB):
-            window = held.tile([P, S], F32, name=f"window{b}")
-            nc.sync.dma_start(window[:], base[b * P : (b + 1) * P, :])
-            windows.append(window)
+        wv_halves = [held.tile([P, KB, C // 2], BF16, name=f"wv_half{g}") for g in range(2)]
+        windows = [held.tile([P, S], F32, name=f"window{b}") for b in range(CB)]
+        nc.sync.dma_start(wv_halves[0][:], wv_view[:, :, 0 : C // 2])
+        nc.sync.dma_start(windows[0][:], base[0:P, :])
+        nc.sync.dma_start(wv_halves[1][:], wv_view[:, :, C // 2 : C])
+        for b in range(1, CB):
+            nc.sync.dma_start(windows[b][:], base[b * P : (b + 1) * P, :])
 
         ones = held.tile([P, P], BF16, name="ones")
-        nc.vector.memset(ones[:], 1.0)
+        nc.gpsimd.memset(ones[:], 1.0)
         eps = held.tile([P, 1], F32, name="eps")
-        nc.vector.memset(eps[:], EPS)
+        nc.gpsimd.memset(eps[:], EPS)
+        scratch = held.tile([P, 1], F32, name="scratch")
+        nc.scalar.activation(scratch[:], eps[:], SQRT)
 
         gain = held.tile([P, KB], F32, name="gain")
         nc.vector.tensor_scalar_add(gain[:], lnw_sb[:], 1.0)
-        hs = held.tile([P, KB, N], BF16, name="hs")
-        for k in range(KB):
-            nc.vector.tensor_scalar_mul(hs[:, k, :], h_sb[:, k, :], gain[:, k : k + 1])
 
-        sq = held.tile([P, KB, N], BF16, name="sq")
-        nc.scalar.activation(sq[:], h_sb[:], SQUARE)
+        hs_chunks = []
         ssq = psum.tile([P, N], F32, name="ssq")
-        for k in range(KB):
-            nc.tensor.matmul(ssq[:], ones[:], sq[:, k, :], start=(k == 0), stop=(k == KB - 1))
+        for i in range(HC):
+            sq = held.tile([P, KC, N], BF16, name=f"sq{i}")
+            nc.scalar.activation(sq[:], h_chunks[i][:], SQUARE)
+            hs = held.tile([P, KC, N], BF16, name=f"hs{i}")
+            for kc in range(KC):
+                k = i * KC + kc
+                nc.vector.tensor_scalar_mul(hs[:, kc, :], h_chunks[i][:, kc, :], gain[:, k : k + 1])
+            hs_chunks.append(hs)
+            for kc in range(KC):
+                k = i * KC + kc
+                nc.tensor.matmul(ssq[:], ones[:], sq[:, kc, :], start=(k == 0), stop=(k == KB - 1))
+
         rms = held.tile([P, N], F32, name="rms")
         nc.scalar.activation(rms[:], ssq[:], SQRT, bias=eps[:], scale=1.0 / E)
         r = held.tile([P, N], F32, name="r")
@@ -62,8 +77,8 @@ def tile_gemmaforcausallm_kernel(tc, h, ln_w, wv, base, offs, out):
             for k in range(KB):
                 nc.tensor.matmul(
                     proj[:],
-                    wv_sb[:, k, b * P : (b + 1) * P],
-                    hs[:, k, :],
+                    wv_halves[b // 2][:, k, (b % 2) * P : (b % 2 + 1) * P],
+                    hs_chunks[k // KC][:, k % KC, :],
                     start=(k == 0),
                     stop=(k == KB - 1),
                 )

@@ -14,6 +14,8 @@ CB = C // P
 HC = 4
 KC = KB // HC
 EPS = 1e-6
+WARM_N = 512
+WARM_COUNT = 6
 
 FLOPS = 2 * E * C * N + 2 * E * N
 
@@ -43,12 +45,16 @@ def tile_gemmaforcausallm_kernel(tc, h, ln_w, wv, base, offs, out):
         for b in range(1, CB):
             nc.sync.dma_start(windows[b][:], base[b * P : (b + 1) * P, :])
 
-        ones = held.tile([P, P], BF16, name="ones")
-        nc.gpsimd.memset(ones[:], 1.0)
+        ones = held.tile([P, WARM_N], BF16, name="ones")
+        nc.vector.memset(ones[:], 1.0)
         eps = held.tile([P, 1], F32, name="eps")
         nc.gpsimd.memset(eps[:], EPS)
         scratch = held.tile([P, 1], F32, name="scratch")
         nc.scalar.activation(scratch[:], eps[:], SQRT)
+
+        warm = psum.tile([P, WARM_N], F32, name="warm")
+        for _ in range(WARM_COUNT):
+            nc.tensor.matmul(warm[:], ones[:, 0:P], ones[:], start=True, stop=True)
 
         gain = held.tile([P, KB], F32, name="gain")
         nc.vector.tensor_scalar_add(gain[:], lnw_sb[:], 1.0)
@@ -65,7 +71,7 @@ def tile_gemmaforcausallm_kernel(tc, h, ln_w, wv, base, offs, out):
             hs_chunks.append(hs)
             for kc in range(KC):
                 k = i * KC + kc
-                nc.tensor.matmul(ssq[:], ones[:], sq[:, kc, :], start=(k == 0), stop=(k == KB - 1))
+                nc.tensor.matmul(ssq[:], ones[:, 0:P], sq[:, kc, :], start=(k == 0), stop=(k == KB - 1))
 
         rms = held.tile([P, N], F32, name="rms")
         nc.scalar.activation(rms[:], ssq[:], SQRT, bias=eps[:], scale=1.0 / E)

@@ -13,6 +13,8 @@ KB = E // P
 CB = C // P
 HC = 4
 KC = KB // HC
+WC = 2
+KW = KB // WC
 EPS = 1e-6
 WARM_N = 512
 WARM_COUNT = 6
@@ -37,12 +39,11 @@ def tile_gemmaforcausallm_kernel(tc, h, ln_w, wv, base, offs, out):
             h_chunks.append(h_chunk)
         offsets = held.tile([P, N // 16], U16, name="offsets")
         nc.sync.dma_start(offsets[:], offs)
-        wv_halves = [held.tile([P, KB, C // 2], BF16, name=f"wv_half{g}") for g in range(2)]
+        wv_chunks = [held.tile([P, KW, C], BF16, name=f"wv_chunk{g}") for g in range(WC)]
         windows = [held.tile([P, S], F32, name=f"window{b}") for b in range(CB)]
-        nc.sync.dma_start(wv_halves[0][:], wv_view[:, :, 0 : C // 2])
-        nc.sync.dma_start(windows[0][:], base[0:P, :])
-        nc.sync.dma_start(wv_halves[1][:], wv_view[:, :, C // 2 : C])
-        for b in range(1, CB):
+        for g in range(WC):
+            nc.sync.dma_start(wv_chunks[g][:], wv_view[:, g * KW : (g + 1) * KW, :])
+        for b in range(CB):
             nc.sync.dma_start(windows[b][:], base[b * P : (b + 1) * P, :])
 
         ones = held.tile([P, WARM_N], BF16, name="ones")
@@ -78,17 +79,20 @@ def tile_gemmaforcausallm_kernel(tc, h, ln_w, wv, base, offs, out):
         r = held.tile([P, N], F32, name="r")
         nc.vector.reciprocal(r[:], rms[:])
 
+        projs = [psum.tile([P, N], F32, name=f"proj{b}") for b in range(CB)]
+        for g in range(WC):
+            for b in range(CB):
+                for k in range(g * KW, (g + 1) * KW):
+                    nc.tensor.matmul(
+                        projs[b][:],
+                        wv_chunks[g][:, k % KW, b * P : (b + 1) * P],
+                        hs_chunks[k // KC][:, k % KC, :],
+                        start=(k == 0),
+                        stop=(k == KB - 1),
+                    )
+
         for b in range(CB):
-            proj = psum.tile([P, N], F32, name=f"proj{b}")
-            for k in range(KB):
-                nc.tensor.matmul(
-                    proj[:],
-                    wv_halves[b // 2][:, k, (b % 2) * P : (b % 2 + 1) * P],
-                    hs_chunks[k // KC][:, k % KC, :],
-                    start=(k == 0),
-                    stop=(k == KB - 1),
-                )
             proj_sb = held.tile([P, N], F32, name=f"proj_sb{b}")
-            nc.scalar.copy(proj_sb[:], proj[:])
+            nc.scalar.copy(proj_sb[:], projs[b][:])
             nc.vector.tensor_tensor(windows[b][:].indirect(offsets[:]), proj_sb[:], r[:], MULT)
             nc.sync.dma_start(out[b * P : (b + 1) * P, :], windows[b][:])

@@ -32,11 +32,8 @@ def tile_gemmaforcausallm_kernel(tc, h, ln_w, wv, base, offs, out):
     ):
         lnw_sb = held.tile([P, KB], F32, name="lnw_sb")
         nc.scalar.dma_start(lnw_sb[:], ln_w.rearrange("(p k) o -> p (k o)", k=KB))
-        h_chunks = []
-        for i in range(HC):
-            h_chunk = held.tile([P, KC, N], F32, name=f"h_chunk{i}")
-            nc.sync.dma_start(h_chunk[:], h_view[:, i * KC : (i + 1) * KC, :])
-            h_chunks.append(h_chunk)
+        h_sb = held.tile([P, KB, N], F32, name="h_sb")
+        nc.sync.dma_start(h_sb[:], h_view)
         offsets = held.tile([P, N // 16], U16, name="offsets")
         nc.sync.dma_start(offsets[:], offs)
         wv_chunks = [held.tile([P, KW, C], BF16, name=f"wv_chunk{g}") for g in range(WC)]
@@ -64,11 +61,11 @@ def tile_gemmaforcausallm_kernel(tc, h, ln_w, wv, base, offs, out):
         ssq = psum.tile([P, N], F32, name="ssq")
         for i in range(HC):
             sq = held.tile([P, KC, N], BF16, name=f"sq{i}")
-            nc.scalar.activation(sq[:], h_chunks[i][:], SQUARE)
+            nc.scalar.activation(sq[:], h_sb[:, i * KC : (i + 1) * KC, :], SQUARE)
             hs = held.tile([P, KC, N], BF16, name=f"hs{i}")
             for kc in range(KC):
                 k = i * KC + kc
-                nc.vector.tensor_scalar_mul(hs[:, kc, :], h_chunks[i][:, kc, :], gain[:, k : k + 1])
+                nc.vector.tensor_scalar_mul(hs[:, kc, :], h_sb[:, k, :], gain[:, k : k + 1])
             hs_chunks.append(hs)
             for kc in range(KC):
                 k = i * KC + kc

@@ -34,12 +34,12 @@ def tile_gemmaforcausallm_kernel(tc, h, ln_w, wv, base, offs, out):
         nc.scalar.dma_start(lnw_sb[:], ln_w.rearrange("(p k) o -> p (k o)", k=KB))
         h_sb = held.tile([P, KB, N], F32, name="h_sb")
         nc.sync.dma_start(h_sb[:], h_view)
-        offsets = held.tile([P, N // 16], U16, name="offsets")
-        nc.sync.dma_start(offsets[:], offs)
         wv_chunks = [held.tile([P, KW, C], BF16, name=f"wv_chunk{g}") for g in range(WC)]
         windows = [held.tile([P, S], F32, name=f"window{b}") for b in range(CB)]
         for g in range(WC):
             nc.sync.dma_start(wv_chunks[g][:], wv_view[:, g * KW : (g + 1) * KW, :])
+        offsets = held.tile([P, N // 16], U16, name="offsets")
+        nc.sync.dma_start(offsets[:], offs)
         for b in range(CB):
             nc.sync.dma_start(windows[b][:], base[b * P : (b + 1) * P, :])
 

@@ -13,8 +13,10 @@ KB = E // P
 CB = C // P
 HC = 4
 KC = KB // HC
-WC = 2
-KW = KB // WC
+LATE = 2
+PAIR = 2
+HALF = C // PAIR
+EARLY = [4, 2]
 EPS = 1e-6
 WARM_N = 512
 WARM_COUNT = 6
@@ -29,18 +31,26 @@ def tile_gemmaforcausallm_kernel(tc, h, ln_w, wv, base, offs, out):
     with (
         tc.tile_pool(name="held", bufs=1) as held,
         tc.psum_pool(name="psum", bufs=1) as psum,
+        tc.psum_pool(name="proj_psum", bufs=PAIR) as proj_psum,
     ):
         lnw_sb = held.tile([P, KB], F32, name="lnw_sb")
         nc.scalar.dma_start(lnw_sb[:], ln_w.rearrange("(p k) o -> p (k o)", k=KB))
         h_sb = held.tile([P, KB, N], F32, name="h_sb")
         nc.sync.dma_start(h_sb[:], h_view)
-        wv_chunks = [held.tile([P, KW, C], BF16, name=f"wv_chunk{g}") for g in range(WC)]
+        wv_early = []
+        starts = [0, EARLY[0]]
+        for k0, rows in zip(starts, EARLY):
+            chunk = held.tile([P, rows, C], BF16, name=f"wv_early{k0}")
+            nc.sync.dma_start(chunk[:], wv_view[:, k0 : k0 + rows, :])
+            wv_early.append(chunk)
+        wv_late = [held.tile([P, LATE, HALF], BF16, name=f"wv_late{q}") for q in range(PAIR)]
         windows = [held.tile([P, S], F32, name=f"window{b}") for b in range(CB)]
-        for g in range(WC):
-            nc.sync.dma_start(wv_chunks[g][:], wv_view[:, g * KW : (g + 1) * KW, :])
+        nc.sync.dma_start(wv_late[0][:], wv_view[:, KB - LATE :, 0:HALF])
         offsets = held.tile([P, N // 16], U16, name="offsets")
         nc.sync.dma_start(offsets[:], offs)
         for b in range(CB):
+            if b == PAIR:
+                nc.sync.dma_start(wv_late[1][:], wv_view[:, KB - LATE :, HALF:])
             nc.sync.dma_start(windows[b][:], base[b * P : (b + 1) * P, :])
 
         ones = held.tile([P, WARM_N], BF16, name="ones")
@@ -76,20 +86,31 @@ def tile_gemmaforcausallm_kernel(tc, h, ln_w, wv, base, offs, out):
         r = held.tile([P, N], F32, name="r")
         nc.vector.reciprocal(r[:], rms[:])
 
-        projs = [psum.tile([P, N], F32, name=f"proj{b}") for b in range(CB)]
-        for g in range(WC):
-            for b in range(CB):
-                for k in range(g * KW, (g + 1) * KW):
+        for pair in range(CB // PAIR):
+            blocks = range(pair * PAIR, (pair + 1) * PAIR)
+            projs = [proj_psum.tile([P, N], F32, name=f"proj{b}", tag="proj") for b in blocks]
+            for k0, rows, chunk in zip(starts, EARLY, wv_early):
+                for b, proj in zip(blocks, projs):
+                    for k in range(k0, k0 + rows):
+                        nc.tensor.matmul(
+                            proj[:],
+                            chunk[:, k - k0, b * P : (b + 1) * P],
+                            hs_chunks[k // KC][:, k % KC, :],
+                            start=(k == 0),
+                            stop=False,
+                        )
+            for b, proj in zip(blocks, projs):
+                col = (b % PAIR) * P
+                for k in range(KB - LATE, KB):
                     nc.tensor.matmul(
-                        projs[b][:],
-                        wv_chunks[g][:, k % KW, b * P : (b + 1) * P],
+                        proj[:],
+                        wv_late[pair][:, k - (KB - LATE), col : col + P],
                         hs_chunks[k // KC][:, k % KC, :],
-                        start=(k == 0),
+                        start=False,
                         stop=(k == KB - 1),
                     )
-
-        for b in range(CB):
-            proj_sb = held.tile([P, N], F32, name=f"proj_sb{b}")
-            nc.scalar.copy(proj_sb[:], projs[b][:])
-            nc.vector.tensor_tensor(windows[b][:].indirect(offsets[:]), proj_sb[:], r[:], MULT)
-            nc.sync.dma_start(out[b * P : (b + 1) * P, :], windows[b][:])
+            for b, proj in zip(blocks, projs):
+                proj_sb = held.tile([P, N], F32, name=f"proj_sb{b}")
+                nc.scalar.copy(proj_sb[:], proj[:])
+                nc.vector.tensor_tensor(windows[b][:].indirect(offsets[:]), proj_sb[:], r[:], MULT)
+                nc.sync.dma_start(out[b * P : (b + 1) * P, :], windows[b][:])

@@ -5,7 +5,7 @@ BF16 = mybir.dt.bfloat16
 U16 = mybir.dt.uint16
 MULT = mybir.AluOpType.mult
 SQUARE = mybir.ActivationFunctionType.Square
-SQRT = mybir.ActivationFunctionType.Sqrt
+ABS_RSQRT = mybir.ActivationFunctionType.Abs_reciprocal_sqrt
 
 P = 128
 E, C, S, N = 1024, 512, 512, 128
@@ -58,7 +58,7 @@ def tile_gemmaforcausallm_kernel(tc, h, ln_w, wv, base, offs, out):
         eps = held.tile([P, 1], F32, name="eps")
         nc.gpsimd.memset(eps[:], EPS)
         scratch = held.tile([P, 1], F32, name="scratch")
-        nc.scalar.activation(scratch[:], eps[:], SQRT)
+        nc.scalar.activation(scratch[:], eps[:], ABS_RSQRT)
 
         warm = psum.tile([P, WARM_N], F32, name="warm")
         for _ in range(WARM_COUNT):
@@ -81,10 +81,8 @@ def tile_gemmaforcausallm_kernel(tc, h, ln_w, wv, base, offs, out):
                 k = i * KC + kc
                 nc.tensor.matmul(ssq[:], ones[:, 0:P], sq[:, kc, :], start=(k == 0), stop=(k == KB - 1))
 
-        rms = held.tile([P, N], F32, name="rms")
-        nc.scalar.activation(rms[:], ssq[:], SQRT, bias=eps[:], scale=1.0 / E)
         r = held.tile([P, N], F32, name="r")
-        nc.vector.reciprocal(r[:], rms[:])
+        nc.scalar.activation(r[:], ssq[:], ABS_RSQRT, bias=eps[:], scale=1.0 / E)
 
         for pair in range(CB // PAIR):
             blocks = range(pair * PAIR, (pair + 1) * PAIR)

@@ -19,7 +19,7 @@ HALF = C // PAIR
 EARLY = [4, 2]
 EPS = 1e-6
 WARM_N = 512
-WARM_COUNT = 6
+WARM_COUNT = 4
 
 FLOPS = 2 * E * C * N + 2 * E * N
 

@@ -87,25 +87,22 @@ def tile_gemmaforcausallm_kernel(tc, h, ln_w, wv, base, offs, out):
         for pair in range(CB // PAIR):
             blocks = range(pair * PAIR, (pair + 1) * PAIR)
             projs = [proj_psum.tile([P, N], F32, name=f"proj{b}", tag="proj") for b in blocks]
-            for k0, rows, chunk in zip(starts, EARLY, wv_early):
-                for b, proj in zip(blocks, projs):
-                    for k in range(k0, k0 + rows):
-                        nc.tensor.matmul(
-                            proj[:],
-                            chunk[:, k - k0, b * P : (b + 1) * P],
-                            hs_chunks[k // KC][:, k % KC, :],
-                            start=(k == 0),
-                            stop=False,
-                        )
             for b, proj in zip(blocks, projs):
                 col = (b % PAIR) * P
-                for k in range(KB - LATE, KB):
+                early = [
+                    (k0 + row, chunk[:, row, b * P : (b + 1) * P])
+                    for k0, rows, chunk in zip(starts, EARLY, wv_early)
+                    for row in range(rows)
+                ]
+                late = [(KB - LATE + row, wv_late[pair][:, row, col : col + P]) for row in range(LATE)]
+                steps = early + late if b % PAIR == 0 else late + early
+                for step, (k, weights) in enumerate(steps):
                     nc.tensor.matmul(
                         proj[:],
-                        wv_late[pair][:, k - (KB - LATE), col : col + P],
+                        weights,
                         hs_chunks[k // KC][:, k % KC, :],
-                        start=False,
-                        stop=(k == KB - 1),
+                        start=(step == 0),
+                        stop=(step == KB - 1),
                     )
             for b, proj in zip(blocks, projs):
                 proj_sb = held.tile([P, N], F32, name=f"proj_sb{b}")

@@ -13,10 +13,10 @@ KB = E // P
 CB = C // P
 HC = 4
 KC = KB // HC
-LATE = 2
+LATE = 1
 PAIR = 2
 HALF = C // PAIR
-EARLY = [4, 2]
+EARLY = [4, 3]
 EPS = 1e-6
 WARM_N = 512
 WARM_COUNT = 4

import concourse.mybir as mybir

F32 = mybir.dt.float32
BF16 = mybir.dt.bfloat16
U16 = mybir.dt.uint16
MULT = mybir.AluOpType.mult
SQUARE = mybir.ActivationFunctionType.Square
ABS_RSQRT = mybir.ActivationFunctionType.Abs_reciprocal_sqrt

P = 128
E, C, S, N = 1024, 512, 512, 128
KB = E // P
CB = C // P
HC = 4
KC = KB // HC
LATE = 1
PAIR = 2
HALF = C // PAIR
EARLY = [4, 3]
EPS = 1e-6
WARM_N = 512
WARM_COUNT = 4

FLOPS = 2 * E * C * N + 2 * E * N


def tile_gemmaforcausallm_kernel(tc, h, ln_w, wv, base, offs, out):
    nc = tc.nc
    h_view = h.rearrange("(p k) j -> p k j", k=KB)
    wv_view = wv.rearrange("(p k) c -> p k c", k=KB)
    with (
        tc.tile_pool(name="held", bufs=1) as held,
        tc.psum_pool(name="psum", bufs=1) as psum,
        tc.psum_pool(name="proj_psum", bufs=PAIR) as proj_psum,
    ):
        lnw_sb = held.tile([P, KB], F32, name="lnw_sb")
        nc.scalar.dma_start(lnw_sb[:], ln_w.rearrange("(p k) o -> p (k o)", k=KB))
        h_sb = held.tile([P, KB, N], F32, name="h_sb")
        nc.sync.dma_start(h_sb[:], h_view)
        wv_early = []
        starts = [0, EARLY[0]]
        for k0, rows in zip(starts, EARLY):
            chunk = held.tile([P, rows, C], BF16, name=f"wv_early{k0}")
            nc.sync.dma_start(chunk[:], wv_view[:, k0 : k0 + rows, :])
            wv_early.append(chunk)
        wv_late = [held.tile([P, LATE, HALF], BF16, name=f"wv_late{q}") for q in range(PAIR)]
        windows = [held.tile([P, S], F32, name=f"window{b}") for b in range(CB)]
        nc.sync.dma_start(wv_late[0][:], wv_view[:, KB - LATE :, 0:HALF])
        offsets = held.tile([P, N // 16], U16, name="offsets")
        nc.sync.dma_start(offsets[:], offs)
        for b in range(CB):
            if b == PAIR:
                nc.sync.dma_start(wv_late[1][:], wv_view[:, KB - LATE :, HALF:])
            nc.sync.dma_start(windows[b][:], base[b * P : (b + 1) * P, :])

        ones = held.tile([P, WARM_N], BF16, name="ones")
        nc.vector.memset(ones[:], 1.0)
        eps = held.tile([P, 1], F32, name="eps")
        nc.gpsimd.memset(eps[:], EPS)
        scratch = held.tile([P, 1], F32, name="scratch")
        nc.scalar.activation(scratch[:], eps[:], ABS_RSQRT)

        warm = psum.tile([P, WARM_N], F32, name="warm")
        for _ in range(WARM_COUNT):
            nc.tensor.matmul(warm[:], ones[:, 0:P], ones[:], start=True, stop=True)

        gain = held.tile([P, KB], F32, name="gain")
        nc.vector.tensor_scalar_add(gain[:], lnw_sb[:], 1.0)

        hs_chunks = []
        ssq = psum.tile([P, N], F32, name="ssq")
        for i in range(HC):
            sq = held.tile([P, KC, N], BF16, name=f"sq{i}")
            nc.scalar.activation(sq[:], h_sb[:, i * KC : (i + 1) * KC, :], SQUARE)
            hs = held.tile([P, KC, N], BF16, name=f"hs{i}")
            for kc in range(KC):
                k = i * KC + kc
                nc.vector.tensor_scalar_mul(hs[:, kc, :], h_sb[:, k, :], gain[:, k : k + 1])
            hs_chunks.append(hs)
            for kc in range(KC):
                k = i * KC + kc
                nc.tensor.matmul(ssq[:], ones[:, 0:P], sq[:, kc, :], start=(k == 0), stop=(k == KB - 1))

        r = held.tile([P, N], F32, name="r")
        nc.scalar.activation(r[:], ssq[:], ABS_RSQRT, bias=eps[:], scale=1.0 / E)

        for pair in range(CB // PAIR):
            blocks = range(pair * PAIR, (pair + 1) * PAIR)
            projs = [proj_psum.tile([P, N], F32, name=f"proj{b}", tag="proj") for b in blocks]
            for b, proj in zip(blocks, projs):
                col = (b % PAIR) * P
                early = [
                    (k0 + row, chunk[:, row, b * P : (b + 1) * P])
                    for k0, rows, chunk in zip(starts, EARLY, wv_early)
                    for row in range(rows)
                ]
                late = [(KB - LATE + row, wv_late[pair][:, row, col : col + P]) for row in range(LATE)]
                steps = early + late if b % PAIR == 0 else late + early
                for step, (k, weights) in enumerate(steps):
                    nc.tensor.matmul(
                        proj[:],
                        weights,
                        hs_chunks[k // KC][:, k % KC, :],
                        start=(step == 0),
                        stop=(step == KB - 1),
                    )
            for b, proj in zip(blocks, projs):
                proj_sb = held.tile([P, N], F32, name=f"proj_sb{b}")
                nc.scalar.copy(proj_sb[:], proj[:])
                nc.vector.tensor_tensor(windows[b][:].indirect(offsets[:]), proj_sb[:], r[:], MULT)
                nc.sync.dma_start(out[b * P : (b + 1) * P, :], windows[b][:])
